import numpy as np
import ml_dtypes


def mxq(x, axis, fmt="e4m3"):
    dtype, down = {"e4m3": (ml_dtypes.float8_e4m3fn, 7), "e5m2": (ml_dtypes.float8_e5m2, 14)}[fmt]
    v = np.moveaxis(np.asarray(x, np.float32).astype(ml_dtypes.bfloat16).astype(np.float64), axis, -1)
    blocks = v.reshape(v.shape[:-1] + (-1, 32))
    amax = np.abs(blocks).max(-1, keepdims=True)
    byte = np.maximum(np.where(amax > 0, np.frexp(amax)[1] - 1 + 127, 0) - down, 1)
    scale = np.exp2(byte - 127.0)
    codes = (blocks / scale).astype(np.float32).astype(dtype).astype(np.float64)
    return np.moveaxis((codes * scale).reshape(v.shape), -1, axis)


WIDE = False


def mx_kscale(k):
    if not WIDE:
        return np.ones(k)
    levels = np.array([10, -10, 5, -5, 0])
    if k % 512:
        return np.exp2(np.random.permutation(np.resize(levels, k // 32))).repeat(32)
    a = np.empty((k // 512, 16))
    for p in range(k // 512):
        a[p, :8] = np.random.permutation(np.resize(levels, 8))
        for g in range(8):
            far = levels[np.abs(levels - a[p, g]) >= 10]
            a[p, g + 8] = far[np.random.randint(len(far))]
    return np.exp2(a.ravel()).repeat(32)


BF16 = ml_dtypes.bfloat16


def bf(x):
    return np.asarray(x, np.float32).astype(BF16)


def f64(x):
    return np.asarray(x).astype(np.float64)


M, K, N, D = 1536, 1536, 1536, 128
GAMMA, ALPHA = 0.5, 0.1


def setup_inputs():
    s, t = mx_kscale(K), mx_kscale(N)
    return {"support0": bf(np.random.standard_normal((M, K)) / np.sqrt(K) * s),
            "f": bf(1.0 + 0.1 * np.random.standard_normal(K)),
            "support1": bf(np.random.standard_normal((K, N)) / np.sqrt(N) / s[:, None] * t),
            "adj": bf(np.random.standard_normal((M, N)) / np.sqrt(N) * t),
            "x": bf(np.random.standard_normal((N, D)) / t[:, None]),
            "h0": bf(np.random.standard_normal((M, D)))}


def reference(support0, f, support1, adj, x, h0):
    a = f64(support0) * f64(f)[None, :]
    bala2 = mxq(a, 1, "e4m3") @ mxq(f64(support1), 0, "e4m3")
    bala3 = GAMMA * bala2 + (1.0 - GAMMA) * f64(adj)
    hi = mxq(bala3, 1, "e4m3") @ mxq(f64(x), 0, "e4m3")
    return (1.0 - ALPHA) * hi + ALPHA * f64(h0)

@@ -1,0 +1,371 @@
+from contextlib import ExitStack
+
+import concourse.mybir as mybir
+from concourse.masks import make_identity
+
+F32 = mybir.dt.float32
+BF16 = mybir.dt.bfloat16
+I32 = mybir.dt.int32
+U32 = mybir.dt.uint32
+U8 = mybir.dt.uint8
+FP8X4 = mybir.dt.float8_e4m3fn_x4
+ADD = mybir.AluOpType.add
+MULT = mybir.AluOpType.mult
+COPY = mybir.ActivationFunctionType.Copy
+
+P = 128
+SIZE = 1536
+D = 128
+PASS = 512
+HALF = 256
+N_PASS = SIZE // PASS
+PAIR = 256
+N_PAIR = SIZE // PAIR
+N_STEP = N_PASS * N_PAIR
+LOAD_BLOCK_1_AFTER = 3
+REGROUP_FROM = 2
+SECOND_LAG = 4
+
+GAMMA = 0.5
+ALPHA = 0.1
+
+FLOPS = 2 * SIZE * SIZE * SIZE + 2 * SIZE * SIZE * D
+
+
+def tile_combinelayer_pa_kernel(tc, support0, f, support1, adj, x, h0, out):
+    nc = tc.nc
+    with ExitStack() as ctx:
+        const = ctx.enter_context(tc.tile_pool(name="const", bufs=1))
+        keep = ctx.enter_context(tc.tile_pool(name="keep", bufs=1))
+        stage = ctx.enter_context(tc.tile_pool(name="stage", bufs=4))
+        turned = ctx.enter_context(tc.psum_pool(name="turned", bufs=4))
+        sums = ctx.enter_context(tc.psum_pool(name="sums", bufs=4))
+
+        ident = const.tile([P, P], F32, name="ident")
+        make_identity(nc, ident[:])
+
+        ctx.enter_context(tc.manual_schedule())
+
+
+        f_rows = const.tile([P, PASS], BF16, name="f_rows")
+        nc.vector.memset(f_rows[:].bitcast(I32), 0)
+        nc.scalar.dma_start(out=f_rows[0:N_PASS, :], in_=f.rearrange("(h w) -> h w", w=PASS))
+        f_bank = turned.tile([P, 2 * PAIR], F32, name="f_bank", tag="turned")
+        for u in range(2):
+            nc.tensor.transpose(f_bank[:, u * P : (u + 1) * P], f_rows[:].bitcast(F32)[:, u:HALF:2], ident[:])
+        f_word = const.tile([P, N_PASS * 4], BF16, name="f_word")
+        nc.vector.tensor_copy(
+            out=f_word[:].bitcast(F32).rearrange("q (c u) -> q c u", u=2),
+            in_=f_bank[:, 0 : 2 * P].rearrange("q (u c) -> q c u", u=2)[:, 0:N_PASS, :],
+        )
+        warm = const.tile([P, 1], F32, name="warm")
+        nc.scalar.activation(out=warm[:], in_=ident[:, 0:1], func=COPY, scale=1.0)
+
+        s0_rows = {}
+        s1_rows = {}
+        adj_rows = {}
+
+        def load_support0(pair):
+            rows = keep.tile([P, 2 * SIZE], BF16, name="s0_rows%d" % pair)
+            nc.sync.dma_start(
+                out=rows[:].rearrange("p (j k) -> p j k", j=2),
+                in_=support0[pair * PAIR : (pair + 1) * PAIR, :].rearrange("(j p) k -> p j k", p=P),
+            )
+            s0_rows[pair] = rows
+
+        def load_support1(block):
+            rows = keep.tile([P, N_PASS * 4 * PASS], BF16, name="s1_rows", tag="s1_rows", bufs=2)
+            view = rows[:].rearrange("q (c t n) -> q c t n", t=4, n=PASS)
+            for c in range(N_PASS):
+                nc.sync.dma_start(
+                    out=view[:, c, :, :],
+                    in_=support1[
+                        c * PASS : (c + 1) * PASS, block * PASS : (block + 1) * PASS
+                    ].rearrange("(q t) n -> q t n", t=4),
+                )
+            s1_rows[block] = rows
+
+        def load_adj(block, pair):
+            rows = keep.tile([P, 2 * PASS], BF16, name="adj_rows%d_%d" % (block, pair))
+            nc.sync.dma_start(
+                out=rows[:].rearrange("p (j n) -> p j n", j=2),
+                in_=adj[
+                    pair * PAIR : (pair + 1) * PAIR, block * PASS : (block + 1) * PASS
+                ].rearrange("(j p) n -> p j n", p=P),
+            )
+            adj_rows[(block, pair)] = rows
+
+        x_rows = keep.tile([P, N_PASS * 4 * D], BF16, name="x_rows")
+        h0_rows = keep.tile([P, (SIZE // P) * D], BF16, name="h0_rows")
+
+        def load_x_h0():
+            nc.sync.dma_start(
+                out=x_rows[:].rearrange("q (c t d) -> q c t d", t=4, d=D),
+                in_=x.rearrange("(c q t) d -> q c t d", q=P, t=4),
+            )
+            nc.sync.dma_start(
+                out=h0_rows[:].rearrange("p (j d) -> p j d", d=D),
+                in_=h0.rearrange("(j p) d -> p j d", p=P),
+            )
+
+        s1_codes = {}
+        s1_scales = {}
+        s1_grouped = {}
+        for block in range(N_PASS):
+            s1_codes[block] = keep.tile([P, N_PASS * PASS], U32, name="s1_codes%d" % block, align_bytes=64)
+            s1_scales[block] = keep.tile([P, N_PASS * PASS], U8, name="s1_scales%d" % block, align_bytes=64)
+
+        def regroup_support1(block, c, on_vector):
+            rows = s1_rows[block][:].rearrange("q (c t w r) -> q c w r t", c=N_PASS, t=4, r=4)
+            grouped = stage.tile([P, 4 * PASS], BF16, name="s1_grouped", tag="s1_grouped", bufs=3, align_bytes=64)
+            view = grouped[:].rearrange("q (r w t) -> q w r t", r=4, t=4)
+            if on_vector:
+                nc.vector.tensor_copy(out=view, in_=rows[:, c])
+            else:
+                nc.scalar.copy(out=view, in_=rows[:, c])
+            s1_grouped[(block, c)] = grouped
+
+        def quantise_support1(block, c):
+            nc.vector.quantize_mx(
+                out=s1_codes[block][:, c * PASS : (c + 1) * PASS].bitcast(FP8X4),
+                scales=s1_scales[block][:, c * PASS : (c + 1) * PASS],
+                in_=s1_grouped[(block, c)][:],
+            )
+
+        a_codes = {}
+        a_scales = {}
+        a_grouped = {}
+        for pair in range(N_PAIR):
+            a_codes[pair] = keep.tile([P, N_PASS * PAIR], U32, name="a_codes%d" % pair, align_bytes=64)
+            a_scales[pair] = keep.tile([P, N_PASS * PAIR], U8, name="a_scales%d" % pair, align_bytes=64)
+
+        def turn_and_scale_support0(pair, c):
+            words = s0_rows[pair][:].bitcast(F32).rearrange("p (j w) -> p j w", j=2)
+            bank = turned.tile([P, 2 * PAIR], F32, name="a_bank", tag="turned")
+            for u in range(2):
+                for j in range(2):
+                    nc.tensor.transpose(
+                        bank[:, u * PAIR + j * P : u * PAIR + (j + 1) * P],
+                        words[:, j, c * HALF + u : (c + 1) * HALF : 2],
+                        ident[:],
+                    )
+            grouped = stage.tile([P, 4 * PAIR], BF16, name="a_grouped", tag="a_grouped", align_bytes=64)
+            nc.vector.tensor_tensor(
+                out=grouped[:].rearrange("q (m u e) -> q m u e", u=2, e=2),
+                in0=bank[:].bitcast(BF16).rearrange("q (u m e) -> q m u e", u=2, e=2),
+                in1=f_word[:, 4 * c : 4 * c + 4]
+                .rearrange("q (u e) -> q u e", e=2)
+                .unsqueeze(1)
+                .to_broadcast([P, PAIR, 2, 2]),
+                op=MULT,
+            )
+            a_grouped[(pair, c)] = grouped
+
+        def quantise_a(pair, c):
+            nc.vector.quantize_mx(
+                out=a_codes[pair][:, c * PAIR : (c + 1) * PAIR].bitcast(FP8X4),
+                scales=a_scales[pair][:, c * PAIR : (c + 1) * PAIR],
+                in_=a_grouped[(pair, c)][:],
+            )
+
+        adj_half = {}
+
+        def turn_and_halve_adj(step):
+            block, pair = divmod(step, N_PAIR)
+            words = adj_rows[(block, pair)][:].bitcast(F32).rearrange("p (j w) -> p j w", j=2)
+            bank = turned.tile([P, 2 * PAIR], F32, name="adj_bank", tag="turned")
+            for u in range(2):
+                for j in range(2):
+                    nc.tensor.transpose(
+                        bank[:, u * PAIR + j * P : u * PAIR + (j + 1) * P],
+                        words[:, j, u:HALF:2],
+                        ident[:],
+                    )
+            half = stage.tile([P, 4 * PAIR], BF16, name="adj_half", tag="adj_half")
+            nc.scalar.activation(
+                out=half[:].rearrange("q (m u e) -> q m u e", u=2, e=2),
+                in_=bank[:].bitcast(BF16).rearrange("q (u m e) -> q m u e", u=2, e=2),
+                func=COPY,
+                scale=1.0 - GAMMA,
+            )
+            adj_half[step] = half
+
+        g_codes = {}
+        g_scales = {}
+        g_grouped = {}
+        p_bank = {}
+        for pair in range(N_PAIR):
+            g_codes[pair] = keep.tile([P, N_PASS * PAIR], U32, name="g_codes%d" % pair, align_bytes=64)
+            g_scales[pair] = keep.tile([P, N_PASS * PAIR], U8, name="g_scales%d" % pair, align_bytes=64)
+
+        def first_matmul(step, j):
+            block, pair = divmod(step, N_PAIR)
+            bank = sums.tile([P, 4 * P], F32, name="p_bank", tag="sums")
+            for u in range(2):
+                for e in range(2):
+                    t = 2 * u + e
+                    for c in range(N_PASS):
+                        cols = slice(c * PASS + t * P, c * PASS + (t + 1) * P)
+                        rows = slice(c * PAIR + j * P, c * PAIR + (j + 1) * P)
+                        nc.tensor.matmul_mx(
+                            out=bank[:, t * P : (t + 1) * P],
+                            lhsT=s1_codes[block][:, cols].bitcast(FP8X4),
+                            lhsT_scale=s1_scales[block][:, cols],
+                            rhs=a_codes[pair][:, rows].bitcast(FP8X4),
+                            rhs_scale=a_scales[pair][:, rows],
+                            start=(c == 0),
+                            stop=(c == N_PASS - 1),
+                        )
+            p_bank[(step, j)] = bank
+
+        def blend(step, j):
+            if j == 0:
+                g_grouped[step] = stage.tile(
+                    [P, 4 * PAIR], BF16, name="g_grouped", tag="g_grouped", bufs=N_PAIR + 1, align_bytes=64
+                )
+            nc.vector.scalar_tensor_tensor(
+                out=g_grouped[step][:, j * 4 * P : (j + 1) * 4 * P],
+                in0=p_bank[(step, j)][:].rearrange("q (t m) -> q m t", t=4),
+                scalar=GAMMA,
+                in1=adj_half[step][:, j * 4 * P : (j + 1) * 4 * P],
+                op0=MULT,
+                op1=ADD,
+            )
+
+        def quantise_g(step):
+            block, pair = divmod(step, N_PAIR)
+            nc.vector.quantize_mx(
+                out=g_codes[pair][:, block * PAIR : (block + 1) * PAIR].bitcast(FP8X4),
+                scales=g_scales[pair][:, block * PAIR : (block + 1) * PAIR],
+                in_=g_grouped[step][:],
+            )
+
+        x_codes = keep.tile([P, N_PASS * D], U32, name="x_codes", align_bytes=64)
+        x_scales = keep.tile([P, N_PASS * D], U8, name="x_scales", align_bytes=64)
+        x_grouped = keep.tile([P, N_PASS * 4 * D], BF16, name="x_grouped", align_bytes=64)
+        h0_part = keep.tile([P, (SIZE // P) * D], F32, name="h0_part")
+
+        def regroup_x_scale_h0():
+            nc.scalar.copy(
+                out=x_grouped[:].rearrange("q (c d t) -> q c d t", c=N_PASS, t=4),
+                in_=x_rows[:].rearrange("q (c t d) -> q c d t", c=N_PASS, t=4),
+            )
+            nc.scalar.activation(out=h0_part[:], in_=h0_rows[:], func=COPY, scale=ALPHA)
+
+        def quantise_x():
+            for c in range(N_PASS):
+                nc.vector.quantize_mx(
+                    out=x_codes[:, c * D : (c + 1) * D].bitcast(FP8X4),
+                    scales=x_scales[:, c * D : (c + 1) * D],
+                    in_=x_grouped[:, c * 4 * D : (c + 1) * 4 * D],
+                )
+
+        hi_bank = {}
+
+        def second_matmul(pair):
+            bank = sums.tile([P, 2 * D], F32, name="hi_bank", tag="sums")
+            for j in range(2):
+                for c in range(N_PASS):
+                    cols = slice(c * PAIR + j * P, c * PAIR + (j + 1) * P)
+                    nc.tensor.matmul_mx(
+                        out=bank[:, j * D : (j + 1) * D],
+                        lhsT=g_codes[pair][:, cols].bitcast(FP8X4),
+                        lhsT_scale=g_scales[pair][:, cols],
+                        rhs=x_codes[:, c * D : (c + 1) * D].bitcast(FP8X4),
+                        rhs_scale=x_scales[:, c * D : (c + 1) * D],
+                        start=(c == 0),
+                        stop=(c == N_PASS - 1),
+                    )
+            hi_bank[pair] = bank
+
+        def finish(pair):
+            rows = stage.tile([P, 2 * D], F32, name="out_rows", tag="out_rows", bufs=SECOND_LAG)
+            nc.vector.scalar_tensor_tensor(
+                out=rows[:],
+                in0=hi_bank[pair][:],
+                scalar=1.0 - ALPHA,
+                in1=h0_part[:, pair * 2 * D : (pair + 1) * 2 * D],
+                op0=MULT,
+                op1=ADD,
+            )
+            nc.sync.dma_start(
+                out=out[pair * PAIR : (pair + 1) * PAIR, :].rearrange("(j p) d -> p j d", p=P),
+                in_=rows[:].rearrange("p (j d) -> p j d", d=D),
+            )
+
+        load_support0(0)
+        load_support1(0)
+        load_adj(0, 0)
+        for pair in range(1, N_PAIR):
+            load_support0(pair)
+            load_adj(0, pair)
+            if pair == LOAD_BLOCK_1_AFTER:
+                load_support1(1)
+
+        turn_and_scale_support0(0, 0)
+        turn_and_scale_support0(0, 1)
+        quantise_a(0, 0)
+        turn_and_scale_support0(0, 2)
+        quantise_a(0, 1)
+        regroup_support1(0, 0, False)
+        regroup_support1(0, 1, False)
+        quantise_a(0, 2)
+        regroup_support1(0, 2, True)
+        for c in range(N_PASS):
+            quantise_support1(0, c)
+        turn_and_halve_adj(0)
+
+        load_support1(2)
+        for pair in range(N_PAIR):
+            load_adj(1, pair)
+        load_x_h0()
+        for pair in range(N_PAIR):
+            load_adj(2, pair)
+
+        for step in range(N_STEP):
+            block, pair = divmod(step, N_PAIR)
+            prepare = block == 0 and pair + 1 < N_PAIR
+
+            if prepare:
+                turn_and_scale_support0(pair + 1, 0)
+                turn_and_scale_support0(pair + 1, 1)
+                quantise_a(pair + 1, 0)
+                turn_and_scale_support0(pair + 1, 2)
+                quantise_a(pair + 1, 1)
+            if block == 0:
+                turn_and_halve_adj(step + 1)
+            elif step % 2 == 0:
+                for later in (step + 1, step + 2):
+                    if later < N_STEP:
+                        turn_and_halve_adj(later)
+            first_matmul(step, 0)
+            first_matmul(step, 1)
+            if block == N_PASS - 1 and pair >= SECOND_LAG:
+                second_matmul(pair - SECOND_LAG)
+
+            if REGROUP_FROM <= step < REGROUP_FROM + 2 * N_PASS:
+                regroup_support1(1 + (step - REGROUP_FROM) // N_PASS, (step - REGROUP_FROM) % N_PASS, False)
+            if step == (N_PASS - 1) * N_PAIR:
+                regroup_x_scale_h0()
+
+            blend(step, 0)
+            if prepare:
+                quantise_a(pair + 1, 2)
+            if step - 1 >= N_PAIR:
+                quantise_g(step - 1)
+            if block == 1:
+                quantise_g(step - N_PAIR)
+            if REGROUP_FROM < step <= REGROUP_FROM + 2 * N_PASS:
+                quantise_support1(1 + (step - 1 - REGROUP_FROM) // N_PASS, (step - 1 - REGROUP_FROM) % N_PASS)
+            blend(step, 1)
+            if step == (N_PASS - 1) * N_PAIR + 1:
+                quantise_x()
+            if block == N_PASS - 1 and pair >= SECOND_LAG:
+                finish(pair - SECOND_LAG)
+
+        for pair in range(N_PAIR - SECOND_LAG, N_PAIR - 1):
+            second_matmul(pair)
+        quantise_g(N_STEP - 1)
+        second_matmul(N_PAIR - 1)
+        for pair in range(N_PAIR - SECOND_LAG, N_PAIR):
+            finish(pair)

@@ -22,9 +22,11 @@ N_PASS = SIZE // PASS
 PAIR = 256
 N_PAIR = SIZE // PAIR
 N_STEP = N_PASS * N_PAIR
-LOAD_BLOCK_1_AFTER = 3
-REGROUP_FROM = 2
+TURN_LAG = 2
+QUANT_LAG = 3
 SECOND_LAG = 4
+REGROUP_AT = {1: 1, 2: 6}
+HEAD_SPLIT = 320
 
 GAMMA = 0.5
 ALPHA = 0.1
@@ -49,7 +51,7 @@ def tile_combinelayer_pa_kernel(tc, support0, f, support1, adj, x, h0, out):
 
         f_rows = const.tile([P, PASS], BF16, name="f_rows")
         nc.vector.memset(f_rows[:].bitcast(I32), 0)
-        nc.scalar.dma_start(out=f_rows[0:N_PASS, :], in_=f.rearrange("(h w) -> h w", w=PASS))
+        nc.sync.dma_start(out=f_rows[0:N_PASS, :], in_=f.rearrange("(h w) -> h w", w=PASS))
         f_bank = turned.tile([P, 2 * PAIR], F32, name="f_bank", tag="turned")
         for u in range(2):
             nc.tensor.transpose(f_bank[:, u * P : (u + 1) * P], f_rows[:].bitcast(F32)[:, u:HALF:2], ident[:])
@@ -61,29 +63,34 @@ def tile_combinelayer_pa_kernel(tc, support0, f, support1, adj, x, h0, out):
         warm = const.tile([P, 1], F32, name="warm")
         nc.scalar.activation(out=warm[:], in_=ident[:, 0:1], func=COPY, scale=1.0)
 
-        s0_rows = {}
+        s0_words = {}
         s1_rows = {}
         adj_rows = {}
 
-        def load_support0(pair):
-            rows = keep.tile([P, 2 * SIZE], BF16, name="s0_rows%d" % pair)
+        def load_support0(pair, c0, c1):
+            width = (c1 - c0) * PASS
+            rows = keep.tile([P, 2 * width], BF16, name="s0_rows%d_%d" % (pair, c0))
             nc.sync.dma_start(
                 out=rows[:].rearrange("p (j k) -> p j k", j=2),
-                in_=support0[pair * PAIR : (pair + 1) * PAIR, :].rearrange("(j p) k -> p j k", p=P),
+                in_=support0[pair * PAIR : (pair + 1) * PAIR, c0 * PASS : c1 * PASS].rearrange(
+                    "(j p) k -> p j k", p=P
+                ),
             )
-            s0_rows[pair] = rows
+            for j in range(2):
+                for c in range(c0, c1):
+                    first = j * width + (c - c0) * PASS
+                    s0_words[(j, pair, c)] = rows[:, first : first + PASS].bitcast(F32)
 
-        def load_support1(block):
-            rows = keep.tile([P, N_PASS * 4 * PASS], BF16, name="s1_rows", tag="s1_rows", bufs=2)
-            view = rows[:].rearrange("q (c t n) -> q c t n", t=4, n=PASS)
-            for c in range(N_PASS):
-                nc.sync.dma_start(
-                    out=view[:, c, :, :],
-                    in_=support1[
-                        c * PASS : (c + 1) * PASS, block * PASS : (block + 1) * PASS
-                    ].rearrange("(q t) n -> q t n", t=4),
-                )
-            s1_rows[block] = rows
+        def load_support1(block, c):
+            if block not in s1_rows:
+                s1_rows[block] = keep.tile([P, N_PASS * 4 * PASS], BF16, name="s1_rows", tag="s1_rows", bufs=2)
+            view = s1_rows[block][:].rearrange("q (c t n) -> q c t n", t=4, n=PASS)
+            nc.sync.dma_start(
+                out=view[:, c, :, :],
+                in_=support1[c * PASS : (c + 1) * PASS, block * PASS : (block + 1) * PASS].rearrange(
+                    "(q t) n -> q t n", t=4
+                ),
+            )
 
         def load_adj(block, pair):
             rows = keep.tile([P, 2 * PASS], BF16, name="adj_rows%d_%d" % (block, pair))
@@ -115,15 +122,15 @@ def tile_combinelayer_pa_kernel(tc, support0, f, support1, adj, x, h0, out):
             s1_codes[block] = keep.tile([P, N_PASS * PASS], U32, name="s1_codes%d" % block, align_bytes=64)
             s1_scales[block] = keep.tile([P, N_PASS * PASS], U8, name="s1_scales%d" % block, align_bytes=64)
 
-        def regroup_support1(block, c, on_vector):
-            rows = s1_rows[block][:].rearrange("q (c t w r) -> q c w r t", c=N_PASS, t=4, r=4)
-            grouped = stage.tile([P, 4 * PASS], BF16, name="s1_grouped", tag="s1_grouped", bufs=3, align_bytes=64)
-            view = grouped[:].rearrange("q (r w t) -> q w r t", r=4, t=4)
-            if on_vector:
-                nc.vector.tensor_copy(out=view, in_=rows[:, c])
-            else:
-                nc.scalar.copy(out=view, in_=rows[:, c])
-            s1_grouped[(block, c)] = grouped
+        def regroup_support1(block, c, n0, n1, copy):
+            if (block, c) not in s1_grouped:
+                s1_grouped[(block, c)] = stage.tile(
+                    [P, 4 * PASS], BF16, name="s1_grouped", tag="s1_grouped", bufs=3, align_bytes=64
+                )
+            copy(
+                out=s1_grouped[(block, c)][:].rearrange("q (n t) -> q n t", t=4)[:, n0:n1, :],
+                in_=s1_rows[block][:].rearrange("q (c t n) -> q c n t", c=N_PASS, t=4)[:, c, n0:n1, :],
+            )
 
         def quantise_support1(block, c):
             nc.vector.quantize_mx(
@@ -140,13 +147,12 @@ def tile_combinelayer_pa_kernel(tc, support0, f, support1, adj, x, h0, out):
             a_scales[pair] = keep.tile([P, N_PASS * PAIR], U8, name="a_scales%d" % pair, align_bytes=64)
 
         def turn_and_scale_support0(pair, c):
-            words = s0_rows[pair][:].bitcast(F32).rearrange("p (j w) -> p j w", j=2)
             bank = turned.tile([P, 2 * PAIR], F32, name="a_bank", tag="turned")
             for u in range(2):
                 for j in range(2):
                     nc.tensor.transpose(
                         bank[:, u * PAIR + j * P : u * PAIR + (j + 1) * P],
-                        words[:, j, c * HALF + u : (c + 1) * HALF : 2],
+                        s0_words[(j, pair, c)][:, u:HALF:2],
                         ident[:],
                     )
             grouped = stage.tile([P, 4 * PAIR], BF16, name="a_grouped", tag="a_grouped", align_bytes=64)
@@ -168,69 +174,66 @@ def tile_combinelayer_pa_kernel(tc, support0, f, support1, adj, x, h0, out):
                 in_=a_grouped[(pair, c)][:],
             )
 
-        adj_half = {}
-
-        def turn_and_halve_adj(step):
-            block, pair = divmod(step, N_PAIR)
-            words = adj_rows[(block, pair)][:].bitcast(F32).rearrange("p (j w) -> p j w", j=2)
-            bank = turned.tile([P, 2 * PAIR], F32, name="adj_bank", tag="turned")
-            for u in range(2):
-                for j in range(2):
-                    nc.tensor.transpose(
-                        bank[:, u * PAIR + j * P : u * PAIR + (j + 1) * P],
-                        words[:, j, u:HALF:2],
-                        ident[:],
-                    )
-            half = stage.tile([P, 4 * PAIR], BF16, name="adj_half", tag="adj_half")
-            nc.scalar.activation(
-                out=half[:].rearrange("q (m u e) -> q m u e", u=2, e=2),
-                in_=bank[:].bitcast(BF16).rearrange("q (u m e) -> q m u e", u=2, e=2),
-                func=COPY,
-                scale=1.0 - GAMMA,
-            )
-            adj_half[step] = half
-
         g_codes = {}
         g_scales = {}
-        g_grouped = {}
         p_bank = {}
+        g_rows = {}
+        g_bank = {}
+        g_grouped = {}
         for pair in range(N_PAIR):
             g_codes[pair] = keep.tile([P, N_PASS * PAIR], U32, name="g_codes%d" % pair, align_bytes=64)
             g_scales[pair] = keep.tile([P, N_PASS * PAIR], U8, name="g_scales%d" % pair, align_bytes=64)
 
         def first_matmul(step, j):
             block, pair = divmod(step, N_PAIR)
-            bank = sums.tile([P, 4 * P], F32, name="p_bank", tag="sums")
-            for u in range(2):
-                for e in range(2):
-                    t = 2 * u + e
-                    for c in range(N_PASS):
-                        cols = slice(c * PASS + t * P, c * PASS + (t + 1) * P)
-                        rows = slice(c * PAIR + j * P, c * PAIR + (j + 1) * P)
-                        nc.tensor.matmul_mx(
-                            out=bank[:, t * P : (t + 1) * P],
-                            lhsT=s1_codes[block][:, cols].bitcast(FP8X4),
-                            lhsT_scale=s1_scales[block][:, cols],
-                            rhs=a_codes[pair][:, rows].bitcast(FP8X4),
-                            rhs_scale=a_scales[pair][:, rows],
-                            start=(c == 0),
-                            stop=(c == N_PASS - 1),
-                        )
+            bank = sums.tile([P, PASS], F32, name="p_bank", tag="sums")
+            for c in range(N_PASS):
+                rows = slice(c * PAIR + j * P, c * PAIR + (j + 1) * P)
+                cols = slice(c * PASS, (c + 1) * PASS)
+                nc.tensor.matmul_mx(
+                    out=bank[:],
+                    lhsT=a_codes[pair][:, rows].bitcast(FP8X4),
+                    lhsT_scale=a_scales[pair][:, rows],
+                    rhs=s1_codes[block][:, cols].bitcast(FP8X4),
+                    rhs_scale=s1_scales[block][:, cols],
+                    start=(c == 0),
+                    stop=(c == N_PASS - 1),
+                )
             p_bank[(step, j)] = bank
 
         def blend(step, j):
+            block, pair = divmod(step, N_PAIR)
             if j == 0:
-                g_grouped[step] = stage.tile(
-                    [P, 4 * PAIR], BF16, name="g_grouped", tag="g_grouped", bufs=N_PAIR + 1, align_bytes=64
-                )
-            nc.vector.scalar_tensor_tensor(
-                out=g_grouped[step][:, j * 4 * P : (j + 1) * 4 * P],
-                in0=p_bank[(step, j)][:].rearrange("q (t m) -> q m t", t=4),
-                scalar=GAMMA,
-                in1=adj_half[step][:, j * 4 * P : (j + 1) * 4 * P],
-                op0=MULT,
-                op1=ADD,
+                g_rows[step] = stage.tile([P, 2 * PASS], BF16, name="g_rows", tag="g_rows")
+            cols = slice(j * PASS, (j + 1) * PASS)
+            nc.vector.tensor_tensor(
+                out=g_rows[step][:, cols].rearrange("p (u q e) -> p u q e", u=2, e=2),
+                in0=p_bank[(step, j)][:].rearrange("p (q u e) -> p u q e", u=2, e=2),
+                in1=adj_rows[(block, pair)][:, cols].rearrange("p (q u e) -> p u q e", u=2, e=2),
+                op=ADD,
             )
+
+        def turn_g(step):
+            words = g_rows[step][:].bitcast(F32)
+            bank = turned.tile([P, 2 * PAIR], F32, name="g_bank", tag="turned")
+            for j in range(2):
+                for u in range(2):
+                    nc.tensor.transpose(
+                        bank[:, u * PAIR + j * P : u * PAIR + (j + 1) * P],
+                        words[:, (2 * j + u) * P : (2 * j + u + 1) * P],
+                        ident[:],
+                    )
+            g_bank[step] = bank
+
+        def group_g(step):
+            grouped = stage.tile(
+                [P, 4 * PAIR], BF16, name="g_grouped", tag="g_grouped", bufs=N_PAIR + 2, align_bytes=64
+            )
+            nc.scalar.copy(
+                out=grouped[:].bitcast(F32).rearrange("q (m u) -> q m u", u=2),
+                in_=g_bank[step][:].rearrange("q (u m) -> q m u", u=2),
+            )
+            g_grouped[step] = grouped
 
         def quantise_g(step):
             block, pair = divmod(step, N_PAIR)
@@ -245,11 +248,13 @@ def tile_combinelayer_pa_kernel(tc, support0, f, support1, adj, x, h0, out):
         x_grouped = keep.tile([P, N_PASS * 4 * D], BF16, name="x_grouped", align_bytes=64)
         h0_part = keep.tile([P, (SIZE // P) * D], F32, name="h0_part")
 
-        def regroup_x_scale_h0():
+        def regroup_x():
             nc.scalar.copy(
                 out=x_grouped[:].rearrange("q (c d t) -> q c d t", c=N_PASS, t=4),
                 in_=x_rows[:].rearrange("q (c t d) -> q c d t", c=N_PASS, t=4),
             )
+
+        def scale_h0():
             nc.scalar.activation(out=h0_part[:], in_=h0_rows[:], func=COPY, scale=ALPHA)
 
         def quantise_x():
@@ -283,7 +288,7 @@ def tile_combinelayer_pa_kernel(tc, support0, f, support1, adj, x, h0, out):
             nc.vector.scalar_tensor_tensor(
                 out=rows[:],
                 in0=hi_bank[pair][:],
-                scalar=1.0 - ALPHA,
+                scalar=GAMMA * (1.0 - ALPHA),
                 in1=h0_part[:, pair * 2 * D : (pair + 1) * 2 * D],
                 op0=MULT,
                 op1=ADD,
@@ -293,79 +298,75 @@ def tile_combinelayer_pa_kernel(tc, support0, f, support1, adj, x, h0, out):
                 in_=rows[:].rearrange("p (j d) -> p j d", d=D),
             )
 
-        load_support0(0)
-        load_support1(0)
+        for c in range(N_PASS):
+            load_support0(0, c, c + 1)
+            load_support1(0, c)
         load_adj(0, 0)
         for pair in range(1, N_PAIR):
-            load_support0(pair)
+            load_support0(pair, 0, N_PASS)
             load_adj(0, pair)
-            if pair == LOAD_BLOCK_1_AFTER:
-                load_support1(1)
+            if pair <= N_PASS:
+                load_support1(1, pair - 1)
 
-        turn_and_scale_support0(0, 0)
-        turn_and_scale_support0(0, 1)
-        quantise_a(0, 0)
-        turn_and_scale_support0(0, 2)
-        quantise_a(0, 1)
-        regroup_support1(0, 0, False)
-        regroup_support1(0, 1, False)
-        quantise_a(0, 2)
-        regroup_support1(0, 2, True)
         for c in range(N_PASS):
+            turn_and_scale_support0(0, c)
+            regroup_support1(0, c, HEAD_SPLIT, PASS, nc.scalar.copy)
+            regroup_support1(0, c, 0, HEAD_SPLIT, nc.vector.tensor_copy)
+            quantise_a(0, c)
             quantise_support1(0, c)
-        turn_and_halve_adj(0)
 
-        load_support1(2)
+        for c in range(N_PASS):
+            load_support1(2, c)
         for pair in range(N_PAIR):
             load_adj(1, pair)
         load_x_h0()
         for pair in range(N_PAIR):
             load_adj(2, pair)
 
-        for step in range(N_STEP):
+        def second_ready(step):
+            pair = step - SECOND_LAG - (N_PASS - 1) * N_PAIR
+            return pair if 0 <= pair < N_PAIR else None
+
+        for step in range(N_STEP + SECOND_LAG):
             block, pair = divmod(step, N_PAIR)
             prepare = block == 0 and pair + 1 < N_PAIR
 
             if prepare:
-                turn_and_scale_support0(pair + 1, 0)
-                turn_and_scale_support0(pair + 1, 1)
-                quantise_a(pair + 1, 0)
-                turn_and_scale_support0(pair + 1, 2)
-                quantise_a(pair + 1, 1)
-            if block == 0:
-                turn_and_halve_adj(step + 1)
-            elif step % 2 == 0:
-                for later in (step + 1, step + 2):
-                    if later < N_STEP:
-                        turn_and_halve_adj(later)
-            first_matmul(step, 0)
-            first_matmul(step, 1)
-            if block == N_PASS - 1 and pair >= SECOND_LAG:
-                second_matmul(pair - SECOND_LAG)
+                for c in range(N_PASS):
+                    turn_and_scale_support0(pair + 1, c)
+                    if c > 0:
+                        quantise_a(pair + 1, c - 1)
+            if 0 <= step - TURN_LAG < N_STEP:
+                turn_g(step - TURN_LAG)
+                group_g(step - TURN_LAG)
+            if step < N_STEP:
+                first_matmul(step, 0)
+                first_matmul(step, 1)
+            if second_ready(step) is not None:
+                second_matmul(second_ready(step))
 
-            if REGROUP_FROM <= step < REGROUP_FROM + 2 * N_PASS:
-                regroup_support1(1 + (step - REGROUP_FROM) // N_PASS, (step - REGROUP_FROM) % N_PASS, False)
-            if step == (N_PASS - 1) * N_PAIR:
-                regroup_x_scale_h0()
+            for later in REGROUP_AT:
+                if 0 <= step - REGROUP_AT[later] < N_PASS:
+                    regroup_support1(later, step - REGROUP_AT[later], 0, PASS, nc.scalar.copy)
+            if step == N_PAIR + N_PASS:
+                regroup_x()
+            if step == N_PAIR + N_PASS + 1:
+                scale_h0()
 
-            blend(step, 0)
+            if step < N_STEP:
+                blend(step, 0)
             if prepare:
-                quantise_a(pair + 1, 2)
-            if step - 1 >= N_PAIR:
-                quantise_g(step - 1)
+                quantise_a(pair + 1, N_PASS - 1)
+            for later in REGROUP_AT:
+                if 0 <= step - 1 - REGROUP_AT[later] < N_PASS:
+                    quantise_support1(later, step - 1 - REGROUP_AT[later])
             if block == 1:
                 quantise_g(step - N_PAIR)
-            if REGROUP_FROM < step <= REGROUP_FROM + 2 * N_PASS:
-                quantise_support1(1 + (step - 1 - REGROUP_FROM) // N_PASS, (step - 1 - REGROUP_FROM) % N_PASS)
-            blend(step, 1)
-            if step == (N_PASS - 1) * N_PAIR + 1:
+            if N_PAIR <= step - QUANT_LAG < N_STEP:
+                quantise_g(step - QUANT_LAG)
+            if step == N_PAIR + N_PASS + 2:
                 quantise_x()
-            if block == N_PASS - 1 and pair >= SECOND_LAG:
-                finish(pair - SECOND_LAG)
-
-        for pair in range(N_PAIR - SECOND_LAG, N_PAIR - 1):
-            second_matmul(pair)
-        quantise_g(N_STEP - 1)
-        second_matmul(N_PAIR - 1)
-        for pair in range(N_PAIR - SECOND_LAG, N_PAIR):
-            finish(pair)
+            if step < N_STEP:
+                blend(step, 1)
+            if second_ready(step) is not None:
+                finish(second_ready(step))

@@ -22,11 +22,10 @@ N_PASS = SIZE // PASS
 PAIR = 256
 N_PAIR = SIZE // PAIR
 N_STEP = N_PASS * N_PAIR
-TURN_LAG = 2
-QUANT_LAG = 3
-SECOND_LAG = 4
-REGROUP_AT = {1: 1, 2: 6}
-HEAD_SPLIT = 320
+HEAD_SPLIT = (320, 320, 320)
+AG_BUFS = 4
+GG_BUFS = 9
+GR_BUFS = 4
 
 GAMMA = 0.5
 ALPHA = 0.1
@@ -63,23 +62,24 @@ def tile_combinelayer_pa_kernel(tc, support0, f, support1, adj, x, h0, out):
         warm = const.tile([P, 1], F32, name="warm")
         nc.scalar.activation(out=warm[:], in_=ident[:, 0:1], func=COPY, scale=1.0)
 
-        s0_words = {}
+        s0_first = {}
+        s0_rows = {}
         s1_rows = {}
         adj_rows = {}
 
-        def load_support0(pair, c0, c1):
-            width = (c1 - c0) * PASS
-            rows = keep.tile([P, 2 * width], BF16, name="s0_rows%d_%d" % (pair, c0))
+        def load_support0_first(c):
+            s0_first[c] = keep.tile([P, 2 * PASS], BF16, name="s0_first%d" % c)
             nc.sync.dma_start(
-                out=rows[:].rearrange("p (j k) -> p j k", j=2),
-                in_=support0[pair * PAIR : (pair + 1) * PAIR, c0 * PASS : c1 * PASS].rearrange(
-                    "(j p) k -> p j k", p=P
-                ),
+                out=s0_first[c][:].rearrange("p (j k) -> p j k", j=2),
+                in_=support0[0:PAIR, c * PASS : (c + 1) * PASS].rearrange("(j p) k -> p j k", p=P),
             )
-            for j in range(2):
-                for c in range(c0, c1):
-                    first = j * width + (c - c0) * PASS
-                    s0_words[(j, pair, c)] = rows[:, first : first + PASS].bitcast(F32)
+
+        def load_support0(pair):
+            s0_rows[pair] = keep.tile([P, 2 * SIZE], BF16, name="s0_rows%d" % pair)
+            nc.sync.dma_start(
+                out=s0_rows[pair][:].rearrange("p (j k) -> p j k", j=2),
+                in_=support0[pair * PAIR : (pair + 1) * PAIR, :].rearrange("(j p) k -> p j k", p=P),
+            )
 
         def load_support1(block, c):
             if block not in s1_rows:
@@ -93,7 +93,7 @@ def tile_combinelayer_pa_kernel(tc, support0, f, support1, adj, x, h0, out):
             )
 
         def load_adj(block, pair):
-            rows = keep.tile([P, 2 * PASS], BF16, name="adj_rows%d_%d" % (block, pair))
+            rows = keep.tile([P, 2 * PASS], BF16, name="adj_rows", tag="adj_rows", bufs=N_STEP)
             nc.sync.dma_start(
                 out=rows[:].rearrange("p (j n) -> p j n", j=2),
                 in_=adj[
@@ -115,6 +115,9 @@ def tile_combinelayer_pa_kernel(tc, support0, f, support1, adj, x, h0, out):
                 in_=h0.rearrange("(j p) d -> p j d", p=P),
             )
 
+        def place(step):
+            return divmod(step, N_PAIR)
+
         s1_codes = {}
         s1_scales = {}
         s1_grouped = {}
@@ -132,6 +135,11 @@ def tile_combinelayer_pa_kernel(tc, support0, f, support1, adj, x, h0, out):
                 in_=s1_rows[block][:].rearrange("q (c t n) -> q c n t", c=N_PASS, t=4)[:, c, n0:n1, :],
             )
 
+        def regroup_half(half):
+            block, rest = divmod(half, 2 * N_PASS)
+            n0 = rest % 2 * HALF
+            regroup_support1(1 + block, rest // 2, n0, n0 + HALF, nc.scalar.copy)
+
         def quantise_support1(block, c):
             nc.vector.quantize_mx(
                 out=s1_codes[block][:, c * PASS : (c + 1) * PASS].bitcast(FP8X4),
@@ -146,46 +154,51 @@ def tile_combinelayer_pa_kernel(tc, support0, f, support1, adj, x, h0, out):
             a_codes[pair] = keep.tile([P, N_PASS * PAIR], U32, name="a_codes%d" % pair, align_bytes=64)
             a_scales[pair] = keep.tile([P, N_PASS * PAIR], U8, name="a_scales%d" % pair, align_bytes=64)
 
-        def turn_and_scale_support0(pair, c):
+        def words_to_turn(pair, j, c, u):
+            if pair == 0:
+                rows = s0_first[c][:, j * PASS : (j + 1) * PASS]
+            else:
+                rows = s0_rows[pair][:, j * SIZE + c * PASS : j * SIZE + (c + 1) * PASS]
+            return rows.bitcast(F32)[:, u:HALF:2]
+
+        def turn_and_scale(pair, c, tiles=(0, 1)):
+            width = len(tiles) * P
             bank = turned.tile([P, 2 * PAIR], F32, name="a_bank", tag="turned")
-            for u in range(2):
-                for j in range(2):
-                    nc.tensor.transpose(
-                        bank[:, u * PAIR + j * P : u * PAIR + (j + 1) * P],
-                        s0_words[(j, pair, c)][:, u:HALF:2],
-                        ident[:],
-                    )
-            grouped = stage.tile([P, 4 * PAIR], BF16, name="a_grouped", tag="a_grouped", align_bytes=64)
+            for n, j in enumerate(tiles):
+                for u in range(2):
+                    first = u * width + n * P
+                    nc.tensor.transpose(bank[:, first : first + P], words_to_turn(pair, j, c, u), ident[:])
+            grouped = stage.tile([P, 4 * PAIR], BF16, name="a_grouped", tag="a_grouped", bufs=AG_BUFS, align_bytes=64)
             nc.vector.tensor_tensor(
-                out=grouped[:].rearrange("q (m u e) -> q m u e", u=2, e=2),
-                in0=bank[:].bitcast(BF16).rearrange("q (u m e) -> q m u e", u=2, e=2),
+                out=grouped[:, 0 : 4 * width].rearrange("q (m u e) -> q m u e", u=2, e=2),
+                in0=bank[:, 0 : 2 * width].bitcast(BF16).rearrange("q (u m e) -> q m u e", u=2, e=2),
                 in1=f_word[:, 4 * c : 4 * c + 4]
                 .rearrange("q (u e) -> q u e", e=2)
                 .unsqueeze(1)
-                .to_broadcast([P, PAIR, 2, 2]),
+                .to_broadcast([P, width, 2, 2]),
                 op=MULT,
             )
-            a_grouped[(pair, c)] = grouped
+            a_grouped[(pair, c, tiles)] = grouped
 
-        def quantise_a(pair, c):
+        def quantise_a(pair, c, tiles=(0, 1)):
+            cols = slice(c * PAIR + tiles[0] * P, c * PAIR + (tiles[-1] + 1) * P)
             nc.vector.quantize_mx(
-                out=a_codes[pair][:, c * PAIR : (c + 1) * PAIR].bitcast(FP8X4),
-                scales=a_scales[pair][:, c * PAIR : (c + 1) * PAIR],
-                in_=a_grouped[(pair, c)][:],
+                out=a_codes[pair][:, cols].bitcast(FP8X4),
+                scales=a_scales[pair][:, cols],
+                in_=a_grouped[(pair, c, tiles)][:, 0 : 4 * len(tiles) * P],
             )
 
         g_codes = {}
         g_scales = {}
         p_bank = {}
         g_rows = {}
-        g_bank = {}
         g_grouped = {}
         for pair in range(N_PAIR):
             g_codes[pair] = keep.tile([P, N_PASS * PAIR], U32, name="g_codes%d" % pair, align_bytes=64)
             g_scales[pair] = keep.tile([P, N_PASS * PAIR], U8, name="g_scales%d" % pair, align_bytes=64)
 
         def first_matmul(step, j):
-            block, pair = divmod(step, N_PAIR)
+            block, pair = place(step)
             bank = sums.tile([P, PASS], F32, name="p_bank", tag="sums")
             for c in range(N_PASS):
                 rows = slice(c * PAIR + j * P, c * PAIR + (j + 1) * P)
@@ -202,9 +215,9 @@ def tile_combinelayer_pa_kernel(tc, support0, f, support1, adj, x, h0, out):
             p_bank[(step, j)] = bank
 
         def blend(step, j):
-            block, pair = divmod(step, N_PAIR)
+            block, pair = place(step)
             if j == 0:
-                g_rows[step] = stage.tile([P, 2 * PASS], BF16, name="g_rows", tag="g_rows")
+                g_rows[step] = stage.tile([P, 2 * PASS], BF16, name="g_rows", tag="g_rows", bufs=GR_BUFS)
             cols = slice(j * PASS, (j + 1) * PASS)
             nc.vector.tensor_tensor(
                 out=g_rows[step][:, cols].rearrange("p (u q e) -> p u q e", u=2, e=2),
@@ -213,34 +226,30 @@ def tile_combinelayer_pa_kernel(tc, support0, f, support1, adj, x, h0, out):
                 op=ADD,
             )
 
-        def turn_g(step):
+        def turn_g(step, tiles=(0, 1)):
             words = g_rows[step][:].bitcast(F32)
+            width = len(tiles) * P
             bank = turned.tile([P, 2 * PAIR], F32, name="g_bank", tag="turned")
-            for j in range(2):
+            for n, j in enumerate(tiles):
                 for u in range(2):
+                    first = u * width + n * P
                     nc.tensor.transpose(
-                        bank[:, u * PAIR + j * P : u * PAIR + (j + 1) * P],
-                        words[:, (2 * j + u) * P : (2 * j + u + 1) * P],
-                        ident[:],
+                        bank[:, first : first + P], words[:, (2 * j + u) * P : (2 * j + u + 1) * P], ident[:]
                     )
-            g_bank[step] = bank
-
-        def group_g(step):
-            grouped = stage.tile(
-                [P, 4 * PAIR], BF16, name="g_grouped", tag="g_grouped", bufs=N_PAIR + 2, align_bytes=64
-            )
+            grouped = stage.tile([P, 4 * PAIR], BF16, name="g_grouped", tag="g_grouped", bufs=GG_BUFS, align_bytes=64)
             nc.scalar.copy(
-                out=grouped[:].bitcast(F32).rearrange("q (m u) -> q m u", u=2),
-                in_=g_bank[step][:].rearrange("q (u m) -> q m u", u=2),
+                out=grouped[:].bitcast(F32)[:, 0 : 2 * width].rearrange("q (m u) -> q m u", u=2),
+                in_=bank[:, 0 : 2 * width].rearrange("q (u m) -> q m u", u=2),
             )
-            g_grouped[step] = grouped
+            g_grouped[(step, tiles)] = grouped
 
-        def quantise_g(step):
-            block, pair = divmod(step, N_PAIR)
+        def quantise_g(step, tiles=(0, 1)):
+            block, pair = place(step)
+            cols = slice(block * PAIR + tiles[0] * P, block * PAIR + (tiles[-1] + 1) * P)
             nc.vector.quantize_mx(
-                out=g_codes[pair][:, block * PAIR : (block + 1) * PAIR].bitcast(FP8X4),
-                scales=g_scales[pair][:, block * PAIR : (block + 1) * PAIR],
-                in_=g_grouped[step][:],
+                out=g_codes[pair][:, cols].bitcast(FP8X4),
+                scales=g_scales[pair][:, cols],
+                in_=g_grouped[(step, tiles)][:, 0 : 4 * len(tiles) * P],
             )
 
         x_codes = keep.tile([P, N_PASS * D], U32, name="x_codes", align_bytes=64)
@@ -267,13 +276,13 @@ def tile_combinelayer_pa_kernel(tc, support0, f, support1, adj, x, h0, out):
 
         hi_bank = {}
 
-        def second_matmul(pair):
+        def second_matmul(pair, tiles=(0, 1)):
             bank = sums.tile([P, 2 * D], F32, name="hi_bank", tag="sums")
-            for j in range(2):
+            for n, j in enumerate(tiles):
                 for c in range(N_PASS):
                     cols = slice(c * PAIR + j * P, c * PAIR + (j + 1) * P)
                     nc.tensor.matmul_mx(
-                        out=bank[:, j * D : (j + 1) * D],
+                        out=bank[:, n * D : (n + 1) * D],
                         lhsT=g_codes[pair][:, cols].bitcast(FP8X4),
                         lhsT_scale=g_scales[pair][:, cols],
                         rhs=x_codes[:, c * D : (c + 1) * D].bitcast(FP8X4),
@@ -281,37 +290,41 @@ def tile_combinelayer_pa_kernel(tc, support0, f, support1, adj, x, h0, out):
                         start=(c == 0),
                         stop=(c == N_PASS - 1),
                     )
-            hi_bank[pair] = bank
+            hi_bank[(pair, tiles)] = bank
 
-        def finish(pair):
-            rows = stage.tile([P, 2 * D], F32, name="out_rows", tag="out_rows", bufs=SECOND_LAG)
+        def finish(pair, tiles=(0, 1)):
+            first, width = 2 * pair + tiles[0], len(tiles) * D
+            rows = stage.tile([P, 2 * D], F32, name="out_rows", tag="out_rows", bufs=4)
             nc.vector.scalar_tensor_tensor(
-                out=rows[:],
-                in0=hi_bank[pair][:],
+                out=rows[:, 0:width],
+                in0=hi_bank[(pair, tiles)][:, 0:width],
                 scalar=GAMMA * (1.0 - ALPHA),
-                in1=h0_part[:, pair * 2 * D : (pair + 1) * 2 * D],
+                in1=h0_part[:, first * D : first * D + width],
                 op0=MULT,
                 op1=ADD,
             )
             nc.sync.dma_start(
-                out=out[pair * PAIR : (pair + 1) * PAIR, :].rearrange("(j p) d -> p j d", p=P),
-                in_=rows[:].rearrange("p (j d) -> p j d", d=D),
+                out=out[first * P : (first + len(tiles)) * P, :].rearrange("(j p) d -> p j d", p=P),
+                in_=rows[:, 0:width].rearrange("p (j d) -> p j d", d=D),
             )
 
         for c in range(N_PASS):
-            load_support0(0, c, c + 1)
+            load_support0_first(c)
             load_support1(0, c)
+        load_support0(1)
         load_adj(0, 0)
-        for pair in range(1, N_PAIR):
-            load_support0(pair, 0, N_PASS)
-            load_adj(0, pair)
-            if pair <= N_PASS:
-                load_support1(1, pair - 1)
+        for pair in range(2, N_PAIR):
+            load_support0(pair)
+            load_adj(0, pair - 1)
+            if pair < N_PASS + 2:
+                load_support1(1, pair - 2)
+        load_adj(0, N_PAIR - 1)
 
         for c in range(N_PASS):
-            turn_and_scale_support0(0, c)
-            regroup_support1(0, c, HEAD_SPLIT, PASS, nc.scalar.copy)
-            regroup_support1(0, c, 0, HEAD_SPLIT, nc.vector.tensor_copy)
+            turn_and_scale(0, c)
+            regroup_support1(0, c, HEAD_SPLIT[c], PASS, nc.scalar.copy)
+            if HEAD_SPLIT[c] > 0:
+                regroup_support1(0, c, 0, HEAD_SPLIT[c], nc.vector.tensor_copy)
             quantise_a(0, c)
             quantise_support1(0, c)
 
@@ -323,50 +336,178 @@ def tile_combinelayer_pa_kernel(tc, support0, f, support1, adj, x, h0, out):
         for pair in range(N_PAIR):
             load_adj(2, pair)
 
-        def second_ready(step):
-            pair = step - SECOND_LAG - (N_PASS - 1) * N_PAIR
-            return pair if 0 <= pair < N_PAIR else None
-
-        for step in range(N_STEP + SECOND_LAG):
-            block, pair = divmod(step, N_PAIR)
-            prepare = block == 0 and pair + 1 < N_PAIR
-
-            if prepare:
-                for c in range(N_PASS):
-                    turn_and_scale_support0(pair + 1, c)
-                    if c > 0:
-                        quantise_a(pair + 1, c - 1)
-            if 0 <= step - TURN_LAG < N_STEP:
-                turn_g(step - TURN_LAG)
-                group_g(step - TURN_LAG)
-            if step < N_STEP:
-                first_matmul(step, 0)
-                first_matmul(step, 1)
-            if second_ready(step) is not None:
-                second_matmul(second_ready(step))
-
-            for later in REGROUP_AT:
-                if 0 <= step - REGROUP_AT[later] < N_PASS:
-                    regroup_support1(later, step - REGROUP_AT[later], 0, PASS, nc.scalar.copy)
-            if step == N_PAIR + N_PASS:
-                regroup_x()
-            if step == N_PAIR + N_PASS + 1:
-                scale_h0()
-
-            if step < N_STEP:
-                blend(step, 0)
-            if prepare:
-                quantise_a(pair + 1, N_PASS - 1)
-            for later in REGROUP_AT:
-                if 0 <= step - 1 - REGROUP_AT[later] < N_PASS:
-                    quantise_support1(later, step - 1 - REGROUP_AT[later])
-            if block == 1:
-                quantise_g(step - N_PAIR)
-            if N_PAIR <= step - QUANT_LAG < N_STEP:
-                quantise_g(step - QUANT_LAG)
-            if step == N_PAIR + N_PASS + 2:
-                quantise_x()
-            if step < N_STEP:
-                blend(step, 1)
-            if second_ready(step) is not None:
-                finish(second_ready(step))
+        turn_and_scale(1, 0)
+        turn_and_scale(1, 1)
+        quantise_a(1, 0)
+        turn_and_scale(1, 2)
+        quantise_a(1, 1)
+        first_matmul(0, 0)
+        first_matmul(0, 1)
+        blend(0, 0)
+        quantise_a(1, 2)
+        blend(0, 1)
+        turn_and_scale(2, 0)
+        turn_and_scale(2, 1)
+        quantise_a(2, 0)
+        turn_and_scale(2, 2)
+        quantise_a(2, 1)
+        first_matmul(1, 0)
+        first_matmul(1, 1)
+        blend(1, 0)
+        quantise_a(2, 2)
+        blend(1, 1)
+        regroup_half(0)
+        regroup_half(1)
+        turn_and_scale(3, 0)
+        turn_and_scale(3, 1)
+        quantise_a(3, 0)
+        turn_and_scale(3, 2)
+        quantise_a(3, 1)
+        turn_g(0)
+        first_matmul(2, 0)
+        first_matmul(2, 1)
+        blend(2, 0)
+        quantise_a(3, 2)
+        blend(2, 1)
+        regroup_half(2)
+        regroup_half(3)
+        quantise_support1(1, 0)
+        turn_and_scale(4, 0)
+        turn_and_scale(4, 1)
+        quantise_a(4, 0)
+        turn_and_scale(4, 2)
+        quantise_a(4, 1)
+        turn_g(1)
+        first_matmul(3, 0)
+        first_matmul(3, 1)
+        blend(3, 0)
+        quantise_a(4, 2)
+        blend(3, 1)
+        regroup_half(4)
+        regroup_half(5)
+        quantise_support1(1, 1)
+        turn_and_scale(5, 0)
+        turn_and_scale(5, 1)
+        quantise_a(5, 0)
+        turn_and_scale(5, 2)
+        quantise_a(5, 1)
+        turn_g(2)
+        first_matmul(4, 0)
+        first_matmul(4, 1)
+        blend(4, 0)
+        quantise_a(5, 2)
+        blend(4, 1)
+        quantise_support1(1, 2)
+        turn_g(3)
+        first_matmul(5, 0)
+        first_matmul(5, 1)
+        blend(5, 0)
+        blend(5, 1)
+        first_matmul(6, 0)
+        blend(6, 0)
+        turn_g(4)
+        turn_g(5)
+        quantise_g(0)
+        first_matmul(6, 1)
+        blend(6, 1)
+        regroup_half(6)
+        regroup_half(7)
+        first_matmul(7, 0)
+        blend(7, 0)
+        quantise_g(1)
+        first_matmul(7, 1)
+        blend(7, 1)
+        regroup_half(8)
+        quantise_support1(2, 0)
+        first_matmul(8, 0)
+        blend(8, 0)
+        turn_g(6)
+        turn_g(7)
+        quantise_g(2)
+        first_matmul(8, 1)
+        blend(8, 1)
+        regroup_half(9)
+        first_matmul(9, 0)
+        blend(9, 0)
+        quantise_g(3)
+        first_matmul(9, 1)
+        blend(9, 1)
+        regroup_half(10)
+        quantise_support1(2, 1)
+        regroup_half(11)
+        first_matmul(10, 0)
+        blend(10, 0)
+        quantise_g(4)
+        first_matmul(10, 1)
+        blend(10, 1)
+        quantise_g(6)
+        regroup_x()
+        first_matmul(11, 0)
+        blend(11, 0)
+        turn_g(8)
+        turn_g(9)
+        turn_g(10)
+        quantise_g(5)
+        quantise_support1(2, 2)
+        first_matmul(11, 1)
+        blend(11, 1)
+        quantise_g(7)
+        scale_h0()
+        first_matmul(12, 0)
+        blend(12, 0)
+        quantise_g(8)
+        first_matmul(12, 1)
+        blend(12, 1)
+        quantise_g(9)
+        first_matmul(13, 0)
+        blend(13, 0)
+        quantise_g(10)
+        quantise_x()
+        first_matmul(13, 1)
+        blend(13, 1)
+        first_matmul(14, 0)
+        blend(14, 0)
+        turn_g(11)
+        turn_g(12)
+        turn_g(13)
+        first_matmul(14, 1)
+        blend(14, 1)
+        quantise_g(11)
+        quantise_g(12)
+        first_matmul(15, 0)
+        blend(15, 0)
+        first_matmul(15, 1)
+        blend(15, 1)
+        quantise_g(13)
+        first_matmul(16, 0)
+        blend(16, 0)
+        second_matmul(0)
+        first_matmul(16, 1)
+        blend(16, 1)
+        finish(0)
+        first_matmul(17, 0)
+        blend(17, 0)
+        turn_g(14)
+        turn_g(15)
+        turn_g(16)
+        second_matmul(1)
+        first_matmul(17, 1)
+        quantise_g(14)
+        blend(17, 1)
+        finish(1)
+        quantise_g(15)
+        second_matmul(2)
+        quantise_g(16)
+        finish(2)
+        turn_g(17, (0,))
+        turn_g(17, (1,))
+        second_matmul(3)
+        quantise_g(17, (0,))
+        quantise_g(17, (1,))
+        finish(3)
+        second_matmul(4)
+        finish(4)
+        second_matmul(5, (0,))
+        second_matmul(5, (1,))
+        finish(5, (0,))
+        finish(5, (1,))

@@ -131,8 +131,10 @@ def tile_combinelayer_pa_kernel(tc, support0, f, support1, adj, x, h0, out):
                     [P, 4 * PASS], BF16, name="s1_grouped", tag="s1_grouped", bufs=3, align_bytes=64
                 )
             copy(
-                out=s1_grouped[(block, c)][:].rearrange("q (n t) -> q n t", t=4)[:, n0:n1, :],
-                in_=s1_rows[block][:].rearrange("q (c t n) -> q c n t", c=N_PASS, t=4)[:, c, n0:n1, :],
+                out=s1_grouped[(block, c)][:, 4 * n0 : 4 * n1].rearrange("q (w i t) -> q w t i", i=4, t=4),
+                in_=s1_rows[block][:]
+                .rearrange("q (c t n) -> q c t n", c=N_PASS, t=4)[:, c, :, n0:n1]
+                .rearrange("q t (w i) -> q w t i", i=4),
             )
 
         def regroup_half(half):

from contextlib import ExitStack

import concourse.mybir as mybir
from concourse.masks import make_identity

F32 = mybir.dt.float32
BF16 = mybir.dt.bfloat16
I32 = mybir.dt.int32
U32 = mybir.dt.uint32
U8 = mybir.dt.uint8
FP8X4 = mybir.dt.float8_e4m3fn_x4
ADD = mybir.AluOpType.add
MULT = mybir.AluOpType.mult
COPY = mybir.ActivationFunctionType.Copy

P = 128
SIZE = 1536
D = 128
PASS = 512
HALF = 256
N_PASS = SIZE // PASS
PAIR = 256
N_PAIR = SIZE // PAIR
N_STEP = N_PASS * N_PAIR
HEAD_SPLIT = (320, 320, 320)
AG_BUFS = 4
GG_BUFS = 9
GR_BUFS = 4

GAMMA = 0.5
ALPHA = 0.1

FLOPS = 2 * SIZE * SIZE * SIZE + 2 * SIZE * SIZE * D


def tile_combinelayer_pa_kernel(tc, support0, f, support1, adj, x, h0, out):
    nc = tc.nc
    with ExitStack() as ctx:
        const = ctx.enter_context(tc.tile_pool(name="const", bufs=1))
        keep = ctx.enter_context(tc.tile_pool(name="keep", bufs=1))
        stage = ctx.enter_context(tc.tile_pool(name="stage", bufs=4))
        turned = ctx.enter_context(tc.psum_pool(name="turned", bufs=4))
        sums = ctx.enter_context(tc.psum_pool(name="sums", bufs=4))

        ident = const.tile([P, P], F32, name="ident")
        make_identity(nc, ident[:])

        ctx.enter_context(tc.manual_schedule())


        f_rows = const.tile([P, PASS], BF16, name="f_rows")
        nc.vector.memset(f_rows[:].bitcast(I32), 0)
        nc.sync.dma_start(out=f_rows[0:N_PASS, :], in_=f.rearrange("(h w) -> h w", w=PASS))
        f_bank = turned.tile([P, 2 * PAIR], F32, name="f_bank", tag="turned")
        for u in range(2):
            nc.tensor.transpose(f_bank[:, u * P : (u + 1) * P], f_rows[:].bitcast(F32)[:, u:HALF:2], ident[:])
        f_word = const.tile([P, N_PASS * 4], BF16, name="f_word")
        nc.vector.tensor_copy(
            out=f_word[:].bitcast(F32).rearrange("q (c u) -> q c u", u=2),
            in_=f_bank[:, 0 : 2 * P].rearrange("q (u c) -> q c u", u=2)[:, 0:N_PASS, :],
        )
        warm = const.tile([P, 1], F32, name="warm")
        nc.scalar.activation(out=warm[:], in_=ident[:, 0:1], func=COPY, scale=1.0)

        s0_first = {}
        s0_rows = {}
        s1_rows = {}
        adj_rows = {}

        def load_support0_first(c):
            s0_first[c] = keep.tile([P, 2 * PASS], BF16, name="s0_first%d" % c)
            nc.sync.dma_start(
                out=s0_first[c][:].rearrange("p (j k) -> p j k", j=2),
                in_=support0[0:PAIR, c * PASS : (c + 1) * PASS].rearrange("(j p) k -> p j k", p=P),
            )

        def load_support0(pair):
            s0_rows[pair] = keep.tile([P, 2 * SIZE], BF16, name="s0_rows%d" % pair)
            nc.sync.dma_start(
                out=s0_rows[pair][:].rearrange("p (j k) -> p j k", j=2),
                in_=support0[pair * PAIR : (pair + 1) * PAIR, :].rearrange("(j p) k -> p j k", p=P),
            )

        def load_support1(block, c):
            if block not in s1_rows:
                s1_rows[block] = keep.tile([P, N_PASS * 4 * PASS], BF16, name="s1_rows", tag="s1_rows", bufs=2)
            view = s1_rows[block][:].rearrange("q (c t n) -> q c t n", t=4, n=PASS)
            nc.sync.dma_start(
                out=view[:, c, :, :],
                in_=support1[c * PASS : (c + 1) * PASS, block * PASS : (block + 1) * PASS].rearrange(
                    "(q t) n -> q t n", t=4
                ),
            )

        def load_adj(block, pair):
            rows = keep.tile([P, 2 * PASS], BF16, name="adj_rows", tag="adj_rows", bufs=N_STEP)
            nc.sync.dma_start(
                out=rows[:].rearrange("p (j n) -> p j n", j=2),
                in_=adj[
                    pair * PAIR : (pair + 1) * PAIR, block * PASS : (block + 1) * PASS
                ].rearrange("(j p) n -> p j n", p=P),
            )
            adj_rows[(block, pair)] = rows

        x_rows = keep.tile([P, N_PASS * 4 * D], BF16, name="x_rows")
        h0_rows = keep.tile([P, (SIZE // P) * D], BF16, name="h0_rows")

        def load_x_h0():
            nc.sync.dma_start(
                out=x_rows[:].rearrange("q (c t d) -> q c t d", t=4, d=D),
                in_=x.rearrange("(c q t) d -> q c t d", q=P, t=4),
            )
            nc.sync.dma_start(
                out=h0_rows[:].rearrange("p (j d) -> p j d", d=D),
                in_=h0.rearrange("(j p) d -> p j d", p=P),
            )

        def place(step):
            return divmod(step, N_PAIR)

        s1_codes = {}
        s1_scales = {}
        s1_grouped = {}
        for block in range(N_PASS):
            s1_codes[block] = keep.tile([P, N_PASS * PASS], U32, name="s1_codes%d" % block, align_bytes=64)
            s1_scales[block] = keep.tile([P, N_PASS * PASS], U8, name="s1_scales%d" % block, align_bytes=64)

        def regroup_support1(block, c, n0, n1, copy):
            if (block, c) not in s1_grouped:
                s1_grouped[(block, c)] = stage.tile(
                    [P, 4 * PASS], BF16, name="s1_grouped", tag="s1_grouped", bufs=3, align_bytes=64
                )
            copy(
                out=s1_grouped[(block, c)][:, 4 * n0 : 4 * n1].rearrange("q (w i t) -> q w t i", i=4, t=4),
                in_=s1_rows[block][:]
                .rearrange("q (c t n) -> q c t n", c=N_PASS, t=4)[:, c, :, n0:n1]
                .rearrange("q t (w i) -> q w t i", i=4),
            )

        def regroup_half(half):
            block, rest = divmod(half, 2 * N_PASS)
            n0 = rest % 2 * HALF
            regroup_support1(1 + block, rest // 2, n0, n0 + HALF, nc.scalar.copy)

        def quantise_support1(block, c):
            nc.vector.quantize_mx(
                out=s1_codes[block][:, c * PASS : (c + 1) * PASS].bitcast(FP8X4),
                scales=s1_scales[block][:, c * PASS : (c + 1) * PASS],
                in_=s1_grouped[(block, c)][:],
            )

        a_codes = {}
        a_scales = {}
        a_grouped = {}
        for pair in range(N_PAIR):
            a_codes[pair] = keep.tile([P, N_PASS * PAIR], U32, name="a_codes%d" % pair, align_bytes=64)
            a_scales[pair] = keep.tile([P, N_PASS * PAIR], U8, name="a_scales%d" % pair, align_bytes=64)

        def words_to_turn(pair, j, c, u):
            if pair == 0:
                rows = s0_first[c][:, j * PASS : (j + 1) * PASS]
            else:
                rows = s0_rows[pair][:, j * SIZE + c * PASS : j * SIZE + (c + 1) * PASS]
            return rows.bitcast(F32)[:, u:HALF:2]

        def turn_and_scale(pair, c, tiles=(0, 1)):
            width = len(tiles) * P
            bank = turned.tile([P, 2 * PAIR], F32, name="a_bank", tag="turned")
            for n, j in enumerate(tiles):
                for u in range(2):
                    first = u * width + n * P
                    nc.tensor.transpose(bank[:, first : first + P], words_to_turn(pair, j, c, u), ident[:])
            grouped = stage.tile([P, 4 * PAIR], BF16, name="a_grouped", tag="a_grouped", bufs=AG_BUFS, align_bytes=64)
            nc.vector.tensor_tensor(
                out=grouped[:, 0 : 4 * width].rearrange("q (m u e) -> q m u e", u=2, e=2),
                in0=bank[:, 0 : 2 * width].bitcast(BF16).rearrange("q (u m e) -> q m u e", u=2, e=2),
                in1=f_word[:, 4 * c : 4 * c + 4]
                .rearrange("q (u e) -> q u e", e=2)
                .unsqueeze(1)
                .to_broadcast([P, width, 2, 2]),
                op=MULT,
            )
            a_grouped[(pair, c, tiles)] = grouped

        def quantise_a(pair, c, tiles=(0, 1)):
            cols = slice(c * PAIR + tiles[0] * P, c * PAIR + (tiles[-1] + 1) * P)
            nc.vector.quantize_mx(
                out=a_codes[pair][:, cols].bitcast(FP8X4),
                scales=a_scales[pair][:, cols],
                in_=a_grouped[(pair, c, tiles)][:, 0 : 4 * len(tiles) * P],
            )

        g_codes = {}
        g_scales = {}
        p_bank = {}
        g_rows = {}
        g_grouped = {}
        for pair in range(N_PAIR):
            g_codes[pair] = keep.tile([P, N_PASS * PAIR], U32, name="g_codes%d" % pair, align_bytes=64)
            g_scales[pair] = keep.tile([P, N_PASS * PAIR], U8, name="g_scales%d" % pair, align_bytes=64)

        def first_matmul(step, j):
            block, pair = place(step)
            bank = sums.tile([P, PASS], F32, name="p_bank", tag="sums")
            for c in range(N_PASS):
                rows = slice(c * PAIR + j * P, c * PAIR + (j + 1) * P)
                cols = slice(c * PASS, (c + 1) * PASS)
                nc.tensor.matmul_mx(
                    out=bank[:],
                    lhsT=a_codes[pair][:, rows].bitcast(FP8X4),
                    lhsT_scale=a_scales[pair][:, rows],
                    rhs=s1_codes[block][:, cols].bitcast(FP8X4),
                    rhs_scale=s1_scales[block][:, cols],
                    start=(c == 0),
                    stop=(c == N_PASS - 1),
                )
            p_bank[(step, j)] = bank

        def blend(step, j):
            block, pair = place(step)
            if j == 0:
                g_rows[step] = stage.tile([P, 2 * PASS], BF16, name="g_rows", tag="g_rows", bufs=GR_BUFS)
            cols = slice(j * PASS, (j + 1) * PASS)
            nc.vector.tensor_tensor(
                out=g_rows[step][:, cols].rearrange("p (u q e) -> p u q e", u=2, e=2),
                in0=p_bank[(step, j)][:].rearrange("p (q u e) -> p u q e", u=2, e=2),
                in1=adj_rows[(block, pair)][:, cols].rearrange("p (q u e) -> p u q e", u=2, e=2),
                op=ADD,
            )

        def turn_g(step, tiles=(0, 1)):
            words = g_rows[step][:].bitcast(F32)
            width = len(tiles) * P
            bank = turned.tile([P, 2 * PAIR], F32, name="g_bank", tag="turned")
            for n, j in enumerate(tiles):
                for u in range(2):
                    first = u * width + n * P
                    nc.tensor.transpose(
                        bank[:, first : first + P], words[:, (2 * j + u) * P : (2 * j + u + 1) * P], ident[:]
                    )
            grouped = stage.tile([P, 4 * PAIR], BF16, name="g_grouped", tag="g_grouped", bufs=GG_BUFS, align_bytes=64)
            nc.scalar.copy(
                out=grouped[:].bitcast(F32)[:, 0 : 2 * width].rearrange("q (m u) -> q m u", u=2),
                in_=bank[:, 0 : 2 * width].rearrange("q (u m) -> q m u", u=2),
            )
            g_grouped[(step, tiles)] = grouped

        def quantise_g(step, tiles=(0, 1)):
            block, pair = place(step)
            cols = slice(block * PAIR + tiles[0] * P, block * PAIR + (tiles[-1] + 1) * P)
            nc.vector.quantize_mx(
                out=g_codes[pair][:, cols].bitcast(FP8X4),
                scales=g_scales[pair][:, cols],
                in_=g_grouped[(step, tiles)][:, 0 : 4 * len(tiles) * P],
            )

        x_codes = keep.tile([P, N_PASS * D], U32, name="x_codes", align_bytes=64)
        x_scales = keep.tile([P, N_PASS * D], U8, name="x_scales", align_bytes=64)
        x_grouped = keep.tile([P, N_PASS * 4 * D], BF16, name="x_grouped", align_bytes=64)
        h0_part = keep.tile([P, (SIZE // P) * D], F32, name="h0_part")

        def regroup_x():
            nc.scalar.copy(
                out=x_grouped[:].rearrange("q (c d t) -> q c d t", c=N_PASS, t=4),
                in_=x_rows[:].rearrange("q (c t d) -> q c d t", c=N_PASS, t=4),
            )

        def scale_h0():
            nc.scalar.activation(out=h0_part[:], in_=h0_rows[:], func=COPY, scale=ALPHA)

        def quantise_x():
            for c in range(N_PASS):
                nc.vector.quantize_mx(
                    out=x_codes[:, c * D : (c + 1) * D].bitcast(FP8X4),
                    scales=x_scales[:, c * D : (c + 1) * D],
                    in_=x_grouped[:, c * 4 * D : (c + 1) * 4 * D],
                )

        hi_bank = {}

        def second_matmul(pair, tiles=(0, 1)):
            bank = sums.tile([P, 2 * D], F32, name="hi_bank", tag="sums")
            for n, j in enumerate(tiles):
                for c in range(N_PASS):
                    cols = slice(c * PAIR + j * P, c * PAIR + (j + 1) * P)
                    nc.tensor.matmul_mx(
                        out=bank[:, n * D : (n + 1) * D],
                        lhsT=g_codes[pair][:, cols].bitcast(FP8X4),
                        lhsT_scale=g_scales[pair][:, cols],
                        rhs=x_codes[:, c * D : (c + 1) * D].bitcast(FP8X4),
                        rhs_scale=x_scales[:, c * D : (c + 1) * D],
                        start=(c == 0),
                        stop=(c == N_PASS - 1),
                    )
            hi_bank[(pair, tiles)] = bank

        def finish(pair, tiles=(0, 1)):
            first, width = 2 * pair + tiles[0], len(tiles) * D
            rows = stage.tile([P, 2 * D], F32, name="out_rows", tag="out_rows", bufs=4)
            nc.vector.scalar_tensor_tensor(
                out=rows[:, 0:width],
                in0=hi_bank[(pair, tiles)][:, 0:width],
                scalar=GAMMA * (1.0 - ALPHA),
                in1=h0_part[:, first * D : first * D + width],
                op0=MULT,
                op1=ADD,
            )
            nc.sync.dma_start(
                out=out[first * P : (first + len(tiles)) * P, :].rearrange("(j p) d -> p j d", p=P),
                in_=rows[:, 0:width].rearrange("p (j d) -> p j d", d=D),
            )

        for c in range(N_PASS):
            load_support0_first(c)
            load_support1(0, c)
        load_support0(1)
        load_adj(0, 0)
        for pair in range(2, N_PAIR):
            load_support0(pair)
            load_adj(0, pair - 1)
            if pair < N_PASS + 2:
                load_support1(1, pair - 2)
        load_adj(0, N_PAIR - 1)

        for c in range(N_PASS):
            turn_and_scale(0, c)
            regroup_support1(0, c, HEAD_SPLIT[c], PASS, nc.scalar.copy)
            if HEAD_SPLIT[c] > 0:
                regroup_support1(0, c, 0, HEAD_SPLIT[c], nc.vector.tensor_copy)
            quantise_a(0, c)
            quantise_support1(0, c)

        for c in range(N_PASS):
            load_support1(2, c)
        for pair in range(N_PAIR):
            load_adj(1, pair)
        load_x_h0()
        for pair in range(N_PAIR):
            load_adj(2, pair)

        turn_and_scale(1, 0)
        turn_and_scale(1, 1)
        quantise_a(1, 0)
        turn_and_scale(1, 2)
        quantise_a(1, 1)
        first_matmul(0, 0)
        first_matmul(0, 1)
        blend(0, 0)
        quantise_a(1, 2)
        blend(0, 1)
        turn_and_scale(2, 0)
        turn_and_scale(2, 1)
        quantise_a(2, 0)
        turn_and_scale(2, 2)
        quantise_a(2, 1)
        first_matmul(1, 0)
        first_matmul(1, 1)
        blend(1, 0)
        quantise_a(2, 2)
        blend(1, 1)
        regroup_half(0)
        regroup_half(1)
        turn_and_scale(3, 0)
        turn_and_scale(3, 1)
        quantise_a(3, 0)
        turn_and_scale(3, 2)
        quantise_a(3, 1)
        turn_g(0)
        first_matmul(2, 0)
        first_matmul(2, 1)
        blend(2, 0)
        quantise_a(3, 2)
        blend(2, 1)
        regroup_half(2)
        regroup_half(3)
        quantise_support1(1, 0)
        turn_and_scale(4, 0)
        turn_and_scale(4, 1)
        quantise_a(4, 0)
        turn_and_scale(4, 2)
        quantise_a(4, 1)
        turn_g(1)
        first_matmul(3, 0)
        first_matmul(3, 1)
        blend(3, 0)
        quantise_a(4, 2)
        blend(3, 1)
        regroup_half(4)
        regroup_half(5)
        quantise_support1(1, 1)
        turn_and_scale(5, 0)
        turn_and_scale(5, 1)
        quantise_a(5, 0)
        turn_and_scale(5, 2)
        quantise_a(5, 1)
        turn_g(2)
        first_matmul(4, 0)
        first_matmul(4, 1)
        blend(4, 0)
        quantise_a(5, 2)
        blend(4, 1)
        quantise_support1(1, 2)
        turn_g(3)
        first_matmul(5, 0)
        first_matmul(5, 1)
        blend(5, 0)
        blend(5, 1)
        first_matmul(6, 0)
        blend(6, 0)
        turn_g(4)
        turn_g(5)
        quantise_g(0)
        first_matmul(6, 1)
        blend(6, 1)
        regroup_half(6)
        regroup_half(7)
        first_matmul(7, 0)
        blend(7, 0)
        quantise_g(1)
        first_matmul(7, 1)
        blend(7, 1)
        regroup_half(8)
        quantise_support1(2, 0)
        first_matmul(8, 0)
        blend(8, 0)
        turn_g(6)
        turn_g(7)
        quantise_g(2)
        first_matmul(8, 1)
        blend(8, 1)
        regroup_half(9)
        first_matmul(9, 0)
        blend(9, 0)
        quantise_g(3)
        first_matmul(9, 1)
        blend(9, 1)
        regroup_half(10)
        quantise_support1(2, 1)
        regroup_half(11)
        first_matmul(10, 0)
        blend(10, 0)
        quantise_g(4)
        first_matmul(10, 1)
        blend(10, 1)
        quantise_g(6)
        regroup_x()
        first_matmul(11, 0)
        blend(11, 0)
        turn_g(8)
        turn_g(9)
        turn_g(10)
        quantise_g(5)
        quantise_support1(2, 2)
        first_matmul(11, 1)
        blend(11, 1)
        quantise_g(7)
        scale_h0()
        first_matmul(12, 0)
        blend(12, 0)
        quantise_g(8)
        first_matmul(12, 1)
        blend(12, 1)
        quantise_g(9)
        first_matmul(13, 0)
        blend(13, 0)
        quantise_g(10)
        quantise_x()
        first_matmul(13, 1)
        blend(13, 1)
        first_matmul(14, 0)
        blend(14, 0)
        turn_g(11)
        turn_g(12)
        turn_g(13)
        first_matmul(14, 1)
        blend(14, 1)
        quantise_g(11)
        quantise_g(12)
        first_matmul(15, 0)
        blend(15, 0)
        first_matmul(15, 1)
        blend(15, 1)
        quantise_g(13)
        first_matmul(16, 0)
        blend(16, 0)
        second_matmul(0)
        first_matmul(16, 1)
        blend(16, 1)
        finish(0)
        first_matmul(17, 0)
        blend(17, 0)
        turn_g(14)
        turn_g(15)
        turn_g(16)
        second_matmul(1)
        first_matmul(17, 1)
        quantise_g(14)
        blend(17, 1)
        finish(1)
        quantise_g(15)
        second_matmul(2)
        quantise_g(16)
        finish(2)
        turn_g(17, (0,))
        turn_g(17, (1,))
        second_matmul(3)
        quantise_g(17, (0,))
        quantise_g(17, (1,))
        finish(3)
        second_matmul(4)
        finish(4)
        second_matmul(5, (0,))
        second_matmul(5, (1,))
        finish(5, (0,))
        finish(5, (1,))
